import numpy as np
import ml_dtypes


def mxq(x, axis, fmt="e4m3"):
    dtype, down = {"e4m3": (ml_dtypes.float8_e4m3fn, 7), "e5m2": (ml_dtypes.float8_e5m2, 14)}[fmt]
    v = np.moveaxis(np.asarray(x, np.float32).astype(ml_dtypes.bfloat16).astype(np.float64), axis, -1)
    blocks = v.reshape(v.shape[:-1] + (-1, 32))
    amax = np.abs(blocks).max(-1, keepdims=True)
    byte = np.maximum(np.where(amax > 0, np.frexp(amax)[1] - 1 + 127, 0) - down, 1)
    scale = np.exp2(byte - 127.0)
    codes = (blocks / scale).astype(np.float32).astype(dtype).astype(np.float64)
    return np.moveaxis((codes * scale).reshape(v.shape), -1, axis)


WIDE = False


def mx_kscale(k):
    if not WIDE:
        return np.ones(k)
    levels = np.array([10, -10, 5, -5, 0])
    a = np.random.permutation(np.resize(levels, k // 512 * 4)).reshape(k // 512, 4)
    idx = np.arange(k)
    return np.exp2(a[idx // 512, idx % 128 // 32])


BF16 = ml_dtypes.bfloat16


def bf(x):
    return np.asarray(x, np.float32).astype(BF16)


def f64(x):
    return np.asarray(x).astype(np.float64)


B, L, C, K = 64, 2, 512, 5
F = C
BN_EPS = 1e-3
LEAKY_ALPHA = 0.3


def leaky(v):
    return np.where(v >= 0, v, LEAKY_ALPHA * v)


def bn(v, gamma, beta, mean, var):
    return gamma * (v - mean) * (1.0 / np.sqrt(var + BN_EPS)) + beta


def setup_inputs():
    s = mx_kscale(C)
    return {"x": bf(np.random.standard_normal((B, L, C)) * s),
            "k1": bf(np.random.standard_normal((K, L, C, F)) * 0.14 / np.sqrt(K * C) / s[:, None]),
            "b1": bf(np.random.standard_normal((L, F)) * 0.03),
            "gamma1": bf(1.0 + 0.1 * np.random.standard_normal(F)),
            "beta1": bf(np.random.standard_normal(F) * 0.2),
            "mean1": bf(np.random.standard_normal(F) * 0.05),
            "var1": bf(np.random.uniform(0.01, 0.03, F))}


def reference(x, k1, b1, gamma1, beta1, mean1, var1):
    xq = mxq(f64(x).transpose(1, 0, 2), 2, "e4m3")
    k = f64(k1)
    out = 2.0 * f64(b1)
    for i in range(k.shape[0]):
        step = (i // 2) * (-1 if i % 2 == 1 else 1)
        ki = np.roll(k[i], -step, axis=0) if step != 0 else k[i]
        p = xq @ mxq(ki, 1, "e4m3")
        p = np.roll(p, step, axis=0) if step != 0 else p
        out = out + p.transpose(1, 0, 2)
    return leaky(bn(out, f64(gamma1), f64(beta1), f64(mean1), f64(var1)))

@@ -1,0 +1,190 @@
+from contextlib import ExitStack
+
+import concourse.mybir as mybir
+from concourse.masks import make_identity
+
+BF16 = mybir.dt.bfloat16
+F32 = mybir.dt.float32
+U32 = mybir.dt.uint32
+U8 = mybir.dt.uint8
+FP8X4 = mybir.dt.float8_e4m3fn_x4
+ALU = mybir.AluOpType
+
+P = 128
+PACK = 4
+BATCH, POSITIONS, CHANNELS, FILTERS, TAPS = 64, 2, 512, 512, 5
+TAP_STEP = (0, 0, 1, -1, 2)
+BN_EPS = 1e-3
+LEAKY_ALPHA = 0.3
+FLOPS = 2 * BATCH * POSITIONS * TAPS * CHANNELS * FILTERS
+
+KERNELS = TAPS * POSITIONS
+HALF = FILTERS // 2
+CHUNKS = FILTERS // P
+VARIANTS = 2 * POSITIONS
+
+
+def tile_residualblock5_pa_s_kernel(tc, x, k1, b1, gamma1, beta1, mean1, var1, out):
+    nc = tc.nc
+    with ExitStack() as ctx:
+        keep = ctx.enter_context(tc.tile_pool(name="keep", bufs=1))
+        psum = ctx.enter_context(tc.psum_pool(name="psum", bufs=1))
+
+        ident_f32 = keep.tile([P, P], F32)
+        make_identity(nc, ident_f32[:])
+        ident_bf16 = keep.tile([P, P], BF16)
+        make_identity(nc, ident_bf16[:])
+        minus_half = keep.tile([P, CHUNKS], F32)
+        nc.gpsimd.memset(minus_half[:], -0.5)
+        vec_rows = keep.tile([P, P], BF16)
+        nc.gpsimd.memset(vec_rows[:], 0.0)
+        x_grouped = keep.tile([P, VARIANTS * P * PACK], BF16, align_bytes=64)
+        nc.vector.memset(x_grouped[:], 0.0)
+
+        for row, vec in enumerate((gamma1, beta1, mean1, var1)):
+            nc.scalar.dma_start(
+                out=vec_rows[row * CHUNKS : (row + 1) * CHUNKS, :],
+                in_=vec.rearrange("(c p) -> c p", p=P),
+            )
+        nc.scalar.dma_start(
+            out=vec_rows[4 * CHUNKS : 6 * CHUNKS, :], in_=b1.rearrange("l (c p) -> (l c) p", p=P)
+        )
+        x_rows = keep.tile([P, CHANNELS], BF16)
+        nc.sync.dma_start(out=x_rows[:], in_=x.rearrange("b l c -> (b l) c"))
+        raw = []
+        for n in range(KERNELS):
+            tap, pos = divmod(n, POSITIONS)
+            raw_n = keep.tile([P, PACK, FILTERS], BF16, name="raw%d" % n)
+            nc.sync.dma_start(out=raw_n[:], in_=k1[tap, pos].rearrange("(p t) f -> p t f", t=PACK))
+            raw.append(raw_n)
+
+        x_words = x_rows[:].bitcast(F32).rearrange("r (p u) -> r u p", u=2)
+        x_grouped_words = x_grouped[:].bitcast(F32).rearrange(
+            "p (v b l u) -> p v l b u", v=VARIANTS, b=BATCH, l=POSITIONS, u=2
+        )
+        copy_by = (nc.vector.tensor_copy, nc.scalar.copy)
+        for other in range(2):
+            xT = psum.tile([P, 2, P], F32, name="xT%d" % other)
+            for u in range(2):
+                nc.tensor.transpose(xT[:, u, :], x_words[:, u, :], ident_f32[:])
+            xT_by_pos = xT[:].rearrange("p u (b l) -> p l b u", l=POSITIONS)
+            for pos in range(POSITIONS):
+                copy_by[other](
+                    out=x_grouped_words[:, other * POSITIONS + pos, pos],
+                    in_=xT_by_pos[:, (pos + other) % POSITIONS],
+                )
+        x_codes = keep.tile([P, VARIANTS * P], U32, align_bytes=64)
+        x_scales = keep.tile([P, VARIANTS * P], U8, align_bytes=64)
+        nc.vector.quantize_mx(out=x_codes[:].bitcast(FP8X4), scales=x_scales[:], in_=x_grouped[:])
+
+        vecT = psum.tile([P, P], BF16)
+        nc.tensor.transpose(vecT[:], vec_rows[:], ident_bf16[:])
+        vec_cols = keep.tile([P, 6 * CHUNKS], F32)
+        nc.scalar.copy(out=vec_cols[:], in_=vecT[:, 0 : 6 * CHUNKS])
+        gamma_col = vec_cols[:, 0 * CHUNKS : 1 * CHUNKS]
+        beta_col = vec_cols[:, 1 * CHUNKS : 2 * CHUNKS]
+        mean_col = vec_cols[:, 2 * CHUNKS : 3 * CHUNKS]
+        var_col = vec_cols[:, 3 * CHUNKS : 4 * CHUNKS]
+        bias_col = vec_cols[:, 4 * CHUNKS : 6 * CHUNKS].rearrange("p (l c) -> p l c", l=POSITIONS)
+
+        def both_positions(col):
+            return col.unsqueeze(1).to_broadcast([P, POSITIONS, CHUNKS])
+
+        var_eps = keep.tile([P, CHUNKS], F32)
+        nc.gpsimd.tensor_scalar(
+            out=var_eps[:], in0=var_col, scalar1=BN_EPS, scalar2=1.0, op0=ALU.add, op1=ALU.mult
+        )
+        rstd = keep.tile([P, CHUNKS], F32)
+        nc.gpsimd.tensor_tensor(out=rstd[:], in0=var_eps[:], in1=minus_half[:], op=ALU.pow)
+        scale_col = keep.tile([P, CHUNKS], F32)
+        nc.gpsimd.tensor_tensor(out=scale_col[:], in0=gamma_col, in1=rstd[:], op=ALU.mult)
+        twice_bias = keep.tile([P, POSITIONS, CHUNKS], F32)
+        nc.gpsimd.tensor_scalar(
+            out=twice_bias[:], in0=bias_col, scalar1=2.0, scalar2=0.0, op0=ALU.mult, op1=ALU.add
+        )
+        centred = keep.tile([P, POSITIONS, CHUNKS], F32)
+        nc.gpsimd.tensor_tensor(
+            out=centred[:], in0=twice_bias[:], in1=both_positions(mean_col), op=ALU.subtract
+        )
+        scaled_bias = keep.tile([P, POSITIONS, CHUNKS], F32)
+        nc.gpsimd.tensor_tensor(
+            out=scaled_bias[:], in0=centred[:], in1=both_positions(scale_col[:]), op=ALU.mult
+        )
+        shift_col = keep.tile([P, POSITIONS, CHUNKS], F32)
+        nc.gpsimd.tensor_tensor(
+            out=shift_col[:], in0=scaled_bias[:], in1=both_positions(beta_col), op=ALU.add
+        )
+        shift_rep = keep.tile([P, CHUNKS, BATCH, POSITIONS], F32)
+        nc.scalar.copy(
+            out=shift_rep[:],
+            in_=shift_col[:]
+            .rearrange("p l c -> p c l")
+            .unsqueeze(2)
+            .to_broadcast([P, CHUNKS, BATCH, POSITIONS]),
+        )
+        scale_ps = psum.tile([P, FILTERS], F32)
+        shift_ps = psum.tile([P, FILTERS], F32)
+        for c in range(CHUNKS):
+            cols = slice(c * P, (c + 1) * P)
+            nc.tensor.transpose(
+                scale_ps[:, cols], scale_col[:, c : c + 1].to_broadcast([P, P]), ident_f32[:]
+            )
+            nc.tensor.transpose(
+                shift_ps[:, cols], shift_rep[:, c].rearrange("p b l -> p (b l)"), ident_f32[:]
+            )
+        scale_sb = keep.tile([P, FILTERS], F32)
+        nc.scalar.copy(out=scale_sb[:], in_=scale_ps[:])
+
+        w_codes = keep.tile([P, KERNELS, FILTERS], U32, align_bytes=64)
+        w_scales = keep.tile([P, KERNELS, FILTERS], U8, align_bytes=64)
+        acc = [psum.tile([P, HALF], F32, name="acc%d" % h) for h in range(2)]
+        grouped = {}
+
+        def regroup(n, h):
+            cols = slice(h * HALF, (h + 1) * HALF)
+            grouped[n, h] = keep.tile([P, HALF, PACK], BF16, name="grouped%d_%d" % (n, h), align_bytes=64)
+            copy_by[h](
+                out=grouped[n, h][:].rearrange("p (c i) t -> p c t i", i=4),
+                in_=raw[n][:, :, cols].rearrange("p t (c i) -> p c t i", i=4),
+            )
+
+        def quantise_and_multiply(n, h):
+            tap, pos = divmod(n, POSITIONS)
+            cols = slice(h * HALF, (h + 1) * HALF)
+            nc.vector.quantize_mx(
+                out=w_codes[:, n, cols].bitcast(FP8X4),
+                scales=w_scales[:, n, cols],
+                in_=grouped[n, h][:].rearrange("p f t -> p (f t)"),
+            )
+            variant = (TAP_STEP[tap] % POSITIONS) * POSITIONS + pos
+            rows = slice(variant * P, (variant + 1) * P)
+            nc.tensor.matmul_mx(
+                out=acc[h][:],
+                lhsT=x_codes[:, rows].bitcast(FP8X4),
+                lhsT_scale=x_scales[:, rows],
+                rhs=w_codes[:, n, cols].bitcast(FP8X4),
+                rhs_scale=w_scales[:, n, cols],
+                start=(n == 0),
+                stop=(n == KERNELS - 1),
+            )
+
+        for n in range(KERNELS):
+            regroup(n, 0)
+            regroup(n, 1)
+            if n > 0:
+                quantise_and_multiply(n - 1, 1)
+            quantise_and_multiply(n, 0)
+        quantise_and_multiply(KERNELS - 1, 1)
+
+        out_rows = out.rearrange("b l f -> (b l) f")
+        for h in range(2):
+            cols = slice(h * HALF, (h + 1) * HALF)
+            scaled = keep.tile([P, HALF], F32, name="scaled%d" % h)
+            nc.vector.tensor_tensor(out=scaled[:], in0=acc[h][:], in1=scale_sb[:, cols], op=ALU.mult)
+            z = keep.tile([P, HALF], F32, name="z%d" % h)
+            nc.vector.tensor_tensor(out=z[:], in0=scaled[:], in1=shift_ps[:, cols], op=ALU.add)
+            result = keep.tile([P, HALF], F32, name="result%d" % h)
+            nc.vector.scalar_tensor_tensor(
+                out=result[:], in0=z[:], scalar=LEAKY_ALPHA, in1=z[:], op0=ALU.mult, op1=ALU.max
+            )
+            nc.sync.dma_start(out=out_rows[:, cols], in_=result[:])

@@ -9,6 +9,7 @@ U32 = mybir.dt.uint32
 U8 = mybir.dt.uint8
 FP8X4 = mybir.dt.float8_e4m3fn_x4
 ALU = mybir.AluOpType
+ACT = mybir.ActivationFunctionType
 
 P = 128
 PACK = 4
@@ -22,6 +23,7 @@ KERNELS = TAPS * POSITIONS
 HALF = FILTERS // 2
 CHUNKS = FILTERS // P
 VARIANTS = 2 * POSITIONS
+BN_FIRST = 3
 
 
 def tile_residualblock5_pa_s_kernel(tc, x, k1, b1, gamma1, beta1, mean1, var1, out):
@@ -29,15 +31,17 @@ def tile_residualblock5_pa_s_kernel(tc, x, k1, b1, gamma1, beta1, mean1, var1, o
     with ExitStack() as ctx:
         keep = ctx.enter_context(tc.tile_pool(name="keep", bufs=1))
         psum = ctx.enter_context(tc.psum_pool(name="psum", bufs=1))
+        ctx.enter_context(tc.manual_schedule())
+        copy_by = (nc.vector.tensor_copy, nc.scalar.copy)
 
-        ident_f32 = keep.tile([P, P], F32)
-        make_identity(nc, ident_f32[:])
-        ident_bf16 = keep.tile([P, P], BF16)
-        make_identity(nc, ident_bf16[:])
-        minus_half = keep.tile([P, CHUNKS], F32)
-        nc.gpsimd.memset(minus_half[:], -0.5)
         vec_rows = keep.tile([P, P], BF16)
         nc.gpsimd.memset(vec_rows[:], 0.0)
+        ident_bf16 = keep.tile([P, P], BF16)
+        make_identity(nc, ident_bf16[:])
+        ident_f32 = keep.tile([P, P], F32)
+        make_identity(nc, ident_f32[:])
+        one = keep.tile([P, 1], F32)
+        nc.vector.memset(one[:], 1.0)
         x_grouped = keep.tile([P, VARIANTS * P * PACK], BF16, align_bytes=64)
         nc.vector.memset(x_grouped[:], 0.0)
 
@@ -57,12 +61,13 @@ def tile_residualblock5_pa_s_kernel(tc, x, k1, b1, gamma1, beta1, mean1, var1, o
             raw_n = keep.tile([P, PACK, FILTERS], BF16, name="raw%d" % n)
             nc.sync.dma_start(out=raw_n[:], in_=k1[tap, pos].rearrange("(p t) f -> p t f", t=PACK))
             raw.append(raw_n)
+        warm = keep.tile([P, 1], F32)
+        nc.scalar.activation(out=warm[:], in_=one[:], func=ACT.Abs_reciprocal_sqrt)
 
         x_words = x_rows[:].bitcast(F32).rearrange("r (p u) -> r u p", u=2)
         x_grouped_words = x_grouped[:].bitcast(F32).rearrange(
             "p (v b l u) -> p v l b u", v=VARIANTS, b=BATCH, l=POSITIONS, u=2
         )
-        copy_by = (nc.vector.tensor_copy, nc.scalar.copy)
         for other in range(2):
             xT = psum.tile([P, 2, P], F32, name="xT%d" % other)
             for u in range(2):
@@ -73,67 +78,74 @@ def tile_residualblock5_pa_s_kernel(tc, x, k1, b1, gamma1, beta1, mean1, var1, o
                     out=x_grouped_words[:, other * POSITIONS + pos, pos],
                     in_=xT_by_pos[:, (pos + other) % POSITIONS],
                 )
+
         x_codes = keep.tile([P, VARIANTS * P], U32, align_bytes=64)
         x_scales = keep.tile([P, VARIANTS * P], U8, align_bytes=64)
         nc.vector.quantize_mx(out=x_codes[:].bitcast(FP8X4), scales=x_scales[:], in_=x_grouped[:])
 
-        vecT = psum.tile([P, P], BF16)
-        nc.tensor.transpose(vecT[:], vec_rows[:], ident_bf16[:])
         vec_cols = keep.tile([P, 6 * CHUNKS], F32)
-        nc.scalar.copy(out=vec_cols[:], in_=vecT[:, 0 : 6 * CHUNKS])
         gamma_col = vec_cols[:, 0 * CHUNKS : 1 * CHUNKS]
         beta_col = vec_cols[:, 1 * CHUNKS : 2 * CHUNKS]
         mean_col = vec_cols[:, 2 * CHUNKS : 3 * CHUNKS]
         var_col = vec_cols[:, 3 * CHUNKS : 4 * CHUNKS]
         bias_col = vec_cols[:, 4 * CHUNKS : 6 * CHUNKS].rearrange("p (l c) -> p l c", l=POSITIONS)
+        rstd = keep.tile([P, CHUNKS], F32)
+        scale_col = keep.tile([P, CHUNKS], F32)
+        shift_col = keep.tile([P, POSITIONS, CHUNKS], F32)
+        scale_ps = psum.tile([P, FILTERS], F32)
+        shift_ps = psum.tile([P, FILTERS], F32)
+        scale_sb = keep.tile([P, FILTERS], F32)
 
         def both_positions(col):
             return col.unsqueeze(1).to_broadcast([P, POSITIONS, CHUNKS])
 
-        var_eps = keep.tile([P, CHUNKS], F32)
-        nc.gpsimd.tensor_scalar(
-            out=var_eps[:], in0=var_col, scalar1=BN_EPS, scalar2=1.0, op0=ALU.add, op1=ALU.mult
-        )
-        rstd = keep.tile([P, CHUNKS], F32)
-        nc.gpsimd.tensor_tensor(out=rstd[:], in0=var_eps[:], in1=minus_half[:], op=ALU.pow)
-        scale_col = keep.tile([P, CHUNKS], F32)
-        nc.gpsimd.tensor_tensor(out=scale_col[:], in0=gamma_col, in1=rstd[:], op=ALU.mult)
-        twice_bias = keep.tile([P, POSITIONS, CHUNKS], F32)
-        nc.gpsimd.tensor_scalar(
-            out=twice_bias[:], in0=bias_col, scalar1=2.0, scalar2=0.0, op0=ALU.mult, op1=ALU.add
-        )
-        centred = keep.tile([P, POSITIONS, CHUNKS], F32)
-        nc.gpsimd.tensor_tensor(
-            out=centred[:], in0=twice_bias[:], in1=both_positions(mean_col), op=ALU.subtract
-        )
-        scaled_bias = keep.tile([P, POSITIONS, CHUNKS], F32)
-        nc.gpsimd.tensor_tensor(
-            out=scaled_bias[:], in0=centred[:], in1=both_positions(scale_col[:]), op=ALU.mult
-        )
-        shift_col = keep.tile([P, POSITIONS, CHUNKS], F32)
-        nc.gpsimd.tensor_tensor(
-            out=shift_col[:], in0=scaled_bias[:], in1=both_positions(beta_col), op=ALU.add
-        )
-        shift_rep = keep.tile([P, CHUNKS, BATCH, POSITIONS], F32)
-        nc.scalar.copy(
-            out=shift_rep[:],
-            in_=shift_col[:]
-            .rearrange("p l c -> p c l")
-            .unsqueeze(2)
-            .to_broadcast([P, CHUNKS, BATCH, POSITIONS]),
-        )
-        scale_ps = psum.tile([P, FILTERS], F32)
-        shift_ps = psum.tile([P, FILTERS], F32)
-        for c in range(CHUNKS):
-            cols = slice(c * P, (c + 1) * P)
-            nc.tensor.transpose(
-                scale_ps[:, cols], scale_col[:, c : c + 1].to_broadcast([P, P]), ident_f32[:]
+        def vectors_onto_partitions():
+            vecT = psum.tile([P, P], BF16)
+            nc.tensor.transpose(vecT[:], vec_rows[:], ident_bf16[:])
+            nc.scalar.copy(out=vec_cols[:], in_=vecT[:, 0 : 6 * CHUNKS])
+            nc.scalar.activation(out=rstd[:], in_=var_col, func=ACT.Abs_reciprocal_sqrt, bias=BN_EPS)
+
+        def scale_and_shift():
+            nc.vector.tensor_tensor(out=scale_col[:], in0=gamma_col, in1=rstd[:], op=ALU.mult)
+            centred = keep.tile([P, POSITIONS, CHUNKS], F32)
+            nc.vector.scalar_tensor_tensor(
+                out=centred[:], in0=bias_col, scalar=2.0, in1=both_positions(mean_col),
+                op0=ALU.mult, op1=ALU.subtract,
             )
-            nc.tensor.transpose(
-                shift_ps[:, cols], shift_rep[:, c].rearrange("p b l -> p (b l)"), ident_f32[:]
+            scaled_bias = keep.tile([P, POSITIONS, CHUNKS], F32)
+            nc.vector.tensor_tensor(
+                out=scaled_bias[:], in0=centred[:], in1=both_positions(scale_col[:]), op=ALU.mult
             )
-        scale_sb = keep.tile([P, FILTERS], F32)
-        nc.scalar.copy(out=scale_sb[:], in_=scale_ps[:])
+            nc.vector.tensor_tensor(
+                out=shift_col[:], in0=scaled_bias[:], in1=both_positions(beta_col), op=ALU.add
+            )
+
+        def spread_over_rows():
+            shift_rep = keep.tile([P, CHUNKS, BATCH, POSITIONS], F32)
+            nc.scalar.copy(
+                out=shift_rep[:],
+                in_=shift_col[:]
+                .rearrange("p l c -> p c l")
+                .unsqueeze(2)
+                .to_broadcast([P, CHUNKS, BATCH, POSITIONS]),
+            )
+            for c in range(CHUNKS):
+                nc.tensor.transpose(
+                    scale_ps[:, c * P : (c + 1) * P],
+                    scale_col[:, c : c + 1].to_broadcast([P, P]),
+                    ident_f32[:],
+                )
+            for c in range(CHUNKS):
+                nc.tensor.transpose(
+                    shift_ps[:, c * P : (c + 1) * P],
+                    shift_rep[:, c].rearrange("p b l -> p (b l)"),
+                    ident_f32[:],
+                )
+
+        def scale_into_sbuf():
+            nc.scalar.copy(out=scale_sb[:], in_=scale_ps[:])
+
+        bn_stages = (vectors_onto_partitions, scale_and_shift, spread_over_rows, scale_into_sbuf)
 
         w_codes = keep.tile([P, KERNELS, FILTERS], U32, align_bytes=64)
         w_scales = keep.tile([P, KERNELS, FILTERS], U8, align_bytes=64)
@@ -174,6 +186,8 @@ def tile_residualblock5_pa_s_kernel(tc, x, k1, b1, gamma1, beta1, mean1, var1, o
             if n > 0:
                 quantise_and_multiply(n - 1, 1)
             quantise_and_multiply(n, 0)
+            if BN_FIRST <= n < BN_FIRST + len(bn_stages):
+                bn_stages[n - BN_FIRST]()
         quantise_and_multiply(KERNELS - 1, 1)
 
         out_rows = out.rearrange("b l f -> (b l) f")

@@ -23,7 +23,7 @@ KERNELS = TAPS * POSITIONS
 HALF = FILTERS // 2
 CHUNKS = FILTERS // P
 VARIANTS = 2 * POSITIONS
-BN_FIRST = 3
+BN_FIRST = 2
 
 
 def tile_residualblock5_pa_s_kernel(tc, x, k1, b1, gamma1, beta1, mean1, var1, out):
@@ -91,7 +91,10 @@ def tile_residualblock5_pa_s_kernel(tc, x, k1, b1, gamma1, beta1, mean1, var1, o
         bias_col = vec_cols[:, 4 * CHUNKS : 6 * CHUNKS].rearrange("p (l c) -> p l c", l=POSITIONS)
         rstd = keep.tile([P, CHUNKS], F32)
         scale_col = keep.tile([P, CHUNKS], F32)
+        centred = keep.tile([P, POSITIONS, CHUNKS], F32)
+        scaled_bias = keep.tile([P, POSITIONS, CHUNKS], F32)
         shift_col = keep.tile([P, POSITIONS, CHUNKS], F32)
+        vecT = psum.tile([P, P], BF16)
         scale_ps = psum.tile([P, FILTERS], F32)
         shift_ps = psum.tile([P, FILTERS], F32)
         scale_sb = keep.tile([P, FILTERS], F32)
@@ -100,22 +103,25 @@ def tile_residualblock5_pa_s_kernel(tc, x, k1, b1, gamma1, beta1, mean1, var1, o
             return col.unsqueeze(1).to_broadcast([P, POSITIONS, CHUNKS])
 
         def vectors_onto_partitions():
-            vecT = psum.tile([P, P], BF16)
             nc.tensor.transpose(vecT[:], vec_rows[:], ident_bf16[:])
+
+        def reciprocal_std():
             nc.scalar.copy(out=vec_cols[:], in_=vecT[:, 0 : 6 * CHUNKS])
             nc.scalar.activation(out=rstd[:], in_=var_col, func=ACT.Abs_reciprocal_sqrt, bias=BN_EPS)
 
-        def scale_and_shift():
+        def scale_and_centred_bias():
             nc.vector.tensor_tensor(out=scale_col[:], in0=gamma_col, in1=rstd[:], op=ALU.mult)
-            centred = keep.tile([P, POSITIONS, CHUNKS], F32)
             nc.vector.scalar_tensor_tensor(
                 out=centred[:], in0=bias_col, scalar=2.0, in1=both_positions(mean_col),
                 op0=ALU.mult, op1=ALU.subtract,
             )
-            scaled_bias = keep.tile([P, POSITIONS, CHUNKS], F32)
+
+        def scale_the_bias():
             nc.vector.tensor_tensor(
                 out=scaled_bias[:], in0=centred[:], in1=both_positions(scale_col[:]), op=ALU.mult
             )
+
+        def add_beta():
             nc.vector.tensor_tensor(
                 out=shift_col[:], in0=scaled_bias[:], in1=both_positions(beta_col), op=ALU.add
             )
@@ -145,29 +151,41 @@ def tile_residualblock5_pa_s_kernel(tc, x, k1, b1, gamma1, beta1, mean1, var1, o
         def scale_into_sbuf():
             nc.scalar.copy(out=scale_sb[:], in_=scale_ps[:])
 
-        bn_stages = (vectors_onto_partitions, scale_and_shift, spread_over_rows, scale_into_sbuf)
+        bn_stages = (
+            vectors_onto_partitions,
+            reciprocal_std,
+            scale_and_centred_bias,
+            scale_the_bias,
+            add_beta,
+            spread_over_rows,
+            scale_into_sbuf,
+        )
 
         w_codes = keep.tile([P, KERNELS, FILTERS], U32, align_bytes=64)
         w_scales = keep.tile([P, KERNELS, FILTERS], U8, align_bytes=64)
         acc = [psum.tile([P, HALF], F32, name="acc%d" % h) for h in range(2)]
-        grouped = {}
+        grouped = []
 
-        def regroup(n, h):
-            cols = slice(h * HALF, (h + 1) * HALF)
-            grouped[n, h] = keep.tile([P, HALF, PACK], BF16, name="grouped%d_%d" % (n, h), align_bytes=64)
-            copy_by[h](
-                out=grouped[n, h][:].rearrange("p (c i) t -> p c t i", i=4),
-                in_=raw[n][:, :, cols].rearrange("p t (c i) -> p c t i", i=4),
-            )
+        def regroup(n):
+            grouped_n = keep.tile([P, FILTERS, PACK], BF16, name="grouped%d" % n, align_bytes=64)
+            for h in range(2):
+                cols = slice(h * HALF, (h + 1) * HALF)
+                copy_by[h](
+                    out=grouped_n[:, cols, :].rearrange("p (c i) t -> p c t i", i=4),
+                    in_=raw[n][:, :, cols].rearrange("p t (c i) -> p c t i", i=4),
+                )
+            grouped.append(grouped_n)
 
-        def quantise_and_multiply(n, h):
-            tap, pos = divmod(n, POSITIONS)
-            cols = slice(h * HALF, (h + 1) * HALF)
+        def quantise(n, cols):
             nc.vector.quantize_mx(
                 out=w_codes[:, n, cols].bitcast(FP8X4),
                 scales=w_scales[:, n, cols],
-                in_=grouped[n, h][:].rearrange("p f t -> p (f t)"),
+                in_=grouped[n][:, cols, :].rearrange("p f t -> p (f t)"),
             )
+
+        def multiply(n, h):
+            tap, pos = divmod(n, POSITIONS)
+            cols = slice(h * HALF, (h + 1) * HALF)
             variant = (TAP_STEP[tap] % POSITIONS) * POSITIONS + pos
             rows = slice(variant * P, (variant + 1) * P)
             nc.tensor.matmul_mx(
@@ -181,24 +199,33 @@ def tile_residualblock5_pa_s_kernel(tc, x, k1, b1, gamma1, beta1, mean1, var1, o
             )
 
         for n in range(KERNELS):
-            regroup(n, 0)
-            regroup(n, 1)
+            regroup(n)
             if n > 0:
-                quantise_and_multiply(n - 1, 1)
-            quantise_and_multiply(n, 0)
+                quantise(n - 1, slice(0, FILTERS))
+                multiply(n - 1, 0)
+                multiply(n - 1, 1)
             if BN_FIRST <= n < BN_FIRST + len(bn_stages):
                 bn_stages[n - BN_FIRST]()
-        quantise_and_multiply(KERNELS - 1, 1)
+        for h in range(2):
+            quantise(KERNELS - 1, slice(h * HALF, (h + 1) * HALF))
+            multiply(KERNELS - 1, h)
 
         out_rows = out.rearrange("b l f -> (b l) f")
+        half_cols = [slice(h * HALF, (h + 1) * HALF) for h in range(2)]
+        scaled = [keep.tile([P, HALF], F32, name="scaled%d" % h) for h in range(2)]
+        z = [keep.tile([P, HALF], F32, name="z%d" % h) for h in range(2)]
+        result = [keep.tile([P, HALF], F32, name="result%d" % h) for h in range(2)]
         for h in range(2):
-            cols = slice(h * HALF, (h + 1) * HALF)
-            scaled = keep.tile([P, HALF], F32, name="scaled%d" % h)
-            nc.vector.tensor_tensor(out=scaled[:], in0=acc[h][:], in1=scale_sb[:, cols], op=ALU.mult)
-            z = keep.tile([P, HALF], F32, name="z%d" % h)
-            nc.vector.tensor_tensor(out=z[:], in0=scaled[:], in1=shift_ps[:, cols], op=ALU.add)
-            result = keep.tile([P, HALF], F32, name="result%d" % h)
-            nc.vector.scalar_tensor_tensor(
-                out=result[:], in0=z[:], scalar=LEAKY_ALPHA, in1=z[:], op0=ALU.mult, op1=ALU.max
+            nc.vector.tensor_tensor(
+                out=scaled[h][:], in0=acc[h][:], in1=scale_sb[:, half_cols[h]], op=ALU.mult
             )
-            nc.sync.dma_start(out=out_rows[:, cols], in_=result[:])
+        for h in range(2):
+            nc.vector.tensor_tensor(
+                out=z[h][:], in0=scaled[h][:], in1=shift_ps[:, half_cols[h]], op=ALU.add
+            )
+        for h in range(2):
+            nc.vector.scalar_tensor_tensor(
+                out=result[h][:], in0=z[h][:], scalar=LEAKY_ALPHA, in1=z[h][:],
+                op0=ALU.mult, op1=ALU.max,
+            )
+            nc.sync.dma_start(out=out_rows[:, half_cols[h]], in_=result[h][:])

@@ -21,6 +21,7 @@ FLOPS = 2 * BATCH * POSITIONS * TAPS * CHANNELS * FILTERS
 
 KERNELS = TAPS * POSITIONS
 HALF = FILTERS // 2
+VECTOR_COLS = 272
 CHUNKS = FILTERS // P
 VARIANTS = 2 * POSITIONS
 BN_FIRST = 2
@@ -32,7 +33,6 @@ def tile_residualblock5_pa_s_kernel(tc, x, k1, b1, gamma1, beta1, mean1, var1, o
         keep = ctx.enter_context(tc.tile_pool(name="keep", bufs=1))
         psum = ctx.enter_context(tc.psum_pool(name="psum", bufs=1))
         ctx.enter_context(tc.manual_schedule())
-        copy_by = (nc.vector.tensor_copy, nc.scalar.copy)
 
         vec_rows = keep.tile([P, P], BF16)
         nc.gpsimd.memset(vec_rows[:], 0.0)
@@ -68,20 +68,19 @@ def tile_residualblock5_pa_s_kernel(tc, x, k1, b1, gamma1, beta1, mean1, var1, o
         x_grouped_words = x_grouped[:].bitcast(F32).rearrange(
             "p (v b l u) -> p v l b u", v=VARIANTS, b=BATCH, l=POSITIONS, u=2
         )
+        xT = psum.tile([P, 2, P], F32)
+        for u in range(2):
+            nc.tensor.transpose(xT[:, u, :], x_words[:, u, :], ident_f32[:])
+        xT_by_pos = xT[:].rearrange("p u (b l) -> p l b u", l=POSITIONS)
         for other in range(2):
-            xT = psum.tile([P, 2, P], F32, name="xT%d" % other)
-            for u in range(2):
-                nc.tensor.transpose(xT[:, u, :], x_words[:, u, :], ident_f32[:])
-            xT_by_pos = xT[:].rearrange("p u (b l) -> p l b u", l=POSITIONS)
             for pos in range(POSITIONS):
-                copy_by[other](
+                nc.scalar.copy(
                     out=x_grouped_words[:, other * POSITIONS + pos, pos],
                     in_=xT_by_pos[:, (pos + other) % POSITIONS],
                 )
 
         x_codes = keep.tile([P, VARIANTS * P], U32, align_bytes=64)
         x_scales = keep.tile([P, VARIANTS * P], U8, align_bytes=64)
-        nc.vector.quantize_mx(out=x_codes[:].bitcast(FP8X4), scales=x_scales[:], in_=x_grouped[:])
 
         vec_cols = keep.tile([P, 6 * CHUNKS], F32)
         gamma_col = vec_cols[:, 0 * CHUNKS : 1 * CHUNKS]
@@ -168,9 +167,11 @@ def tile_residualblock5_pa_s_kernel(tc, x, k1, b1, gamma1, beta1, mean1, var1, o
 
         def regroup(n):
             grouped_n = keep.tile([P, FILTERS, PACK], BF16, name="grouped%d" % n, align_bytes=64)
-            for h in range(2):
-                cols = slice(h * HALF, (h + 1) * HALF)
-                copy_by[h](
+            for copy, cols in (
+                (nc.vector.tensor_copy, slice(0, VECTOR_COLS)),
+                (nc.scalar.copy, slice(VECTOR_COLS, FILTERS)),
+            ):
+                copy(
                     out=grouped_n[:, cols, :].rearrange("p (c i) t -> p c t i", i=4),
                     in_=raw[n][:, :, cols].rearrange("p t (c i) -> p c t i", i=4),
                 )
@@ -200,7 +201,11 @@ def tile_residualblock5_pa_s_kernel(tc, x, k1, b1, gamma1, beta1, mean1, var1, o
 
         for n in range(KERNELS):
             regroup(n)
-            if n > 0:
+            if n == 0:
+                nc.vector.quantize_mx(
+                    out=x_codes[:].bitcast(FP8X4), scales=x_scales[:], in_=x_grouped[:]
+                )
+            else:
                 quantise(n - 1, slice(0, FILTERS))
                 multiply(n - 1, 0)
                 multiply(n - 1, 1)

@@ -21,7 +21,6 @@ FLOPS = 2 * BATCH * POSITIONS * TAPS * CHANNELS * FILTERS
 
 KERNELS = TAPS * POSITIONS
 HALF = FILTERS // 2
-VECTOR_COLS = 272
 CHUNKS = FILTERS // P
 VARIANTS = 2 * POSITIONS
 BN_FIRST = 2
@@ -32,7 +31,7 @@ def tile_residualblock5_pa_s_kernel(tc, x, k1, b1, gamma1, beta1, mean1, var1, o
     with ExitStack() as ctx:
         keep = ctx.enter_context(tc.tile_pool(name="keep", bufs=1))
         psum = ctx.enter_context(tc.psum_pool(name="psum", bufs=1))
-        ctx.enter_context(tc.manual_schedule())
+        copy_by = (nc.vector.tensor_copy, nc.scalar.copy)
 
         vec_rows = keep.tile([P, P], BF16)
         nc.gpsimd.memset(vec_rows[:], 0.0)
@@ -68,19 +67,20 @@ def tile_residualblock5_pa_s_kernel(tc, x, k1, b1, gamma1, beta1, mean1, var1, o
         x_grouped_words = x_grouped[:].bitcast(F32).rearrange(
             "p (v b l u) -> p v l b u", v=VARIANTS, b=BATCH, l=POSITIONS, u=2
         )
-        xT = psum.tile([P, 2, P], F32)
-        for u in range(2):
-            nc.tensor.transpose(xT[:, u, :], x_words[:, u, :], ident_f32[:])
-        xT_by_pos = xT[:].rearrange("p u (b l) -> p l b u", l=POSITIONS)
         for other in range(2):
+            xT = psum.tile([P, 2, P], F32, name="xT%d" % other)
+            for u in range(2):
+                nc.tensor.transpose(xT[:, u, :], x_words[:, u, :], ident_f32[:])
+            xT_by_pos = xT[:].rearrange("p u (b l) -> p l b u", l=POSITIONS)
             for pos in range(POSITIONS):
-                nc.scalar.copy(
+                copy_by[other](
                     out=x_grouped_words[:, other * POSITIONS + pos, pos],
                     in_=xT_by_pos[:, (pos + other) % POSITIONS],
                 )
 
         x_codes = keep.tile([P, VARIANTS * P], U32, align_bytes=64)
         x_scales = keep.tile([P, VARIANTS * P], U8, align_bytes=64)
+        nc.vector.quantize_mx(out=x_codes[:].bitcast(FP8X4), scales=x_scales[:], in_=x_grouped[:])
 
         vec_cols = keep.tile([P, 6 * CHUNKS], F32)
         gamma_col = vec_cols[:, 0 * CHUNKS : 1 * CHUNKS]
@@ -167,11 +167,9 @@ def tile_residualblock5_pa_s_kernel(tc, x, k1, b1, gamma1, beta1, mean1, var1, o
 
         def regroup(n):
             grouped_n = keep.tile([P, FILTERS, PACK], BF16, name="grouped%d" % n, align_bytes=64)
-            for copy, cols in (
-                (nc.vector.tensor_copy, slice(0, VECTOR_COLS)),
-                (nc.scalar.copy, slice(VECTOR_COLS, FILTERS)),
-            ):
-                copy(
+            for h in range(2):
+                cols = slice(h * HALF, (h + 1) * HALF)
+                copy_by[h](
                     out=grouped_n[:, cols, :].rearrange("p (c i) t -> p c t i", i=4),
                     in_=raw[n][:, :, cols].rearrange("p t (c i) -> p c t i", i=4),
                 )
@@ -201,11 +199,7 @@ def tile_residualblock5_pa_s_kernel(tc, x, k1, b1, gamma1, beta1, mean1, var1, o
 
         for n in range(KERNELS):
             regroup(n)
-            if n == 0:
-                nc.vector.quantize_mx(
-                    out=x_codes[:].bitcast(FP8X4), scales=x_scales[:], in_=x_grouped[:]
-                )
-            else:
+            if n > 0:
                 quantise(n - 1, slice(0, FILTERS))
                 multiply(n - 1, 0)
                 multiply(n - 1, 1)

@@ -7,6 +7,7 @@ BF16 = mybir.dt.bfloat16
 F32 = mybir.dt.float32
 U32 = mybir.dt.uint32
 U8 = mybir.dt.uint8
+I32 = mybir.dt.int32
 FP8X4 = mybir.dt.float8_e4m3fn_x4
 ALU = mybir.AluOpType
 ACT = mybir.ActivationFunctionType
@@ -22,7 +23,7 @@ FLOPS = 2 * BATCH * POSITIONS * TAPS * CHANNELS * FILTERS
 KERNELS = TAPS * POSITIONS
 HALF = FILTERS // 2
 CHUNKS = FILTERS // P
-VARIANTS = 2 * POSITIONS
+X_BLOCKS = 2 * POSITIONS + 1
 BN_FIRST = 2
 
 
@@ -41,8 +42,13 @@ def tile_residualblock5_pa_s_kernel(tc, x, k1, b1, gamma1, beta1, mean1, var1, o
         make_identity(nc, ident_f32[:])
         one = keep.tile([P, 1], F32)
         nc.vector.memset(one[:], 1.0)
-        x_grouped = keep.tile([P, VARIANTS * P * PACK], BF16, align_bytes=64)
-        nc.vector.memset(x_grouped[:], 0.0)
+        x_grouped = keep.tile([P, POSITIONS, 2, BATCH * PACK], BF16, align_bytes=64)
+        nc.gpsimd.memset(x_grouped[:, :, 0, :], 0.0)
+        x_codes = keep.tile([P, X_BLOCKS * BATCH], U32, align_bytes=64)
+        x_scales = keep.tile([P, X_BLOCKS * BATCH], U8, align_bytes=64)
+        last_block = slice((X_BLOCKS - 1) * BATCH, X_BLOCKS * BATCH)
+        nc.vector.memset(x_codes[:, last_block].bitcast(I32), 0)
+        nc.vector.memset(x_scales[:, last_block].bitcast(I32), 0)
 
         for row, vec in enumerate((gamma1, beta1, mean1, var1)):
             nc.scalar.dma_start(
@@ -64,23 +70,19 @@ def tile_residualblock5_pa_s_kernel(tc, x, k1, b1, gamma1, beta1, mean1, var1, o
         nc.scalar.activation(out=warm[:], in_=one[:], func=ACT.Abs_reciprocal_sqrt)
 
         x_words = x_rows[:].bitcast(F32).rearrange("r (p u) -> r u p", u=2)
-        x_grouped_words = x_grouped[:].bitcast(F32).rearrange(
-            "p (v b l u) -> p v l b u", v=VARIANTS, b=BATCH, l=POSITIONS, u=2
+        xT = psum.tile([P, 2, P], F32)
+        for u in range(2):
+            nc.tensor.transpose(xT[:, u, :], x_words[:, u, :], ident_f32[:])
+        nc.vector.tensor_copy(
+            out=x_grouped[:, :, 1, :].bitcast(F32).rearrange("p l (b u) -> p l b u", u=2),
+            in_=xT[:].rearrange("p u (b l) -> p l b u", l=POSITIONS),
         )
-        for other in range(2):
-            xT = psum.tile([P, 2, P], F32, name="xT%d" % other)
-            for u in range(2):
-                nc.tensor.transpose(xT[:, u, :], x_words[:, u, :], ident_f32[:])
-            xT_by_pos = xT[:].rearrange("p u (b l) -> p l b u", l=POSITIONS)
-            for pos in range(POSITIONS):
-                copy_by[other](
-                    out=x_grouped_words[:, other * POSITIONS + pos, pos],
-                    in_=xT_by_pos[:, (pos + other) % POSITIONS],
-                )
-
-        x_codes = keep.tile([P, VARIANTS * P], U32, align_bytes=64)
-        x_scales = keep.tile([P, VARIANTS * P], U8, align_bytes=64)
-        nc.vector.quantize_mx(out=x_codes[:].bitcast(FP8X4), scales=x_scales[:], in_=x_grouped[:])
+        quantised_blocks = slice(0, (X_BLOCKS - 1) * BATCH)
+        nc.vector.quantize_mx(
+            out=x_codes[:, quantised_blocks].bitcast(FP8X4),
+            scales=x_scales[:, quantised_blocks],
+            in_=x_grouped[:].rearrange("p l z c -> p (l z c)"),
+        )
 
         vec_cols = keep.tile([P, 6 * CHUNKS], F32)
         gamma_col = vec_cols[:, 0 * CHUNKS : 1 * CHUNKS]
@@ -126,13 +128,13 @@ def tile_residualblock5_pa_s_kernel(tc, x, k1, b1, gamma1, beta1, mean1, var1, o
             )
 
         def spread_over_rows():
-            shift_rep = keep.tile([P, CHUNKS, BATCH, POSITIONS], F32)
+            shift_rep = keep.tile([P, CHUNKS, POSITIONS, BATCH], F32)
             nc.scalar.copy(
                 out=shift_rep[:],
                 in_=shift_col[:]
                 .rearrange("p l c -> p c l")
-                .unsqueeze(2)
-                .to_broadcast([P, CHUNKS, BATCH, POSITIONS]),
+                .unsqueeze(3)
+                .to_broadcast([P, CHUNKS, POSITIONS, BATCH]),
             )
             for c in range(CHUNKS):
                 nc.tensor.transpose(
@@ -143,7 +145,7 @@ def tile_residualblock5_pa_s_kernel(tc, x, k1, b1, gamma1, beta1, mean1, var1, o
             for c in range(CHUNKS):
                 nc.tensor.transpose(
                     shift_ps[:, c * P : (c + 1) * P],
-                    shift_rep[:, c].rearrange("p b l -> p (b l)"),
+                    shift_rep[:, c].rearrange("p l b -> p (l b)"),
                     ident_f32[:],
                 )
 
@@ -185,8 +187,9 @@ def tile_residualblock5_pa_s_kernel(tc, x, k1, b1, gamma1, beta1, mean1, var1, o
         def multiply(n, h):
             tap, pos = divmod(n, POSITIONS)
             cols = slice(h * HALF, (h + 1) * HALF)
-            variant = (TAP_STEP[tap] % POSITIONS) * POSITIONS + pos
-            rows = slice(variant * P, (variant + 1) * P)
+            source = (pos - TAP_STEP[tap]) % POSITIONS
+            first = (2 * source + 1 - pos) * BATCH
+            rows = slice(first, first + P)
             nc.tensor.matmul_mx(
                 out=acc[h][:],
                 lhsT=x_codes[:, rows].bitcast(FP8X4),
@@ -209,7 +212,8 @@ def tile_residualblock5_pa_s_kernel(tc, x, k1, b1, gamma1, beta1, mean1, var1, o
             quantise(KERNELS - 1, slice(h * HALF, (h + 1) * HALF))
             multiply(KERNELS - 1, h)
 
-        out_rows = out.rearrange("b l f -> (b l) f")
+        out_by_pos = out.rearrange("b l f -> l b f")
+        store_by = (nc.sync, nc.scalar)
         half_cols = [slice(h * HALF, (h + 1) * HALF) for h in range(2)]
         scaled = [keep.tile([P, HALF], F32, name="scaled%d" % h) for h in range(2)]
         z = [keep.tile([P, HALF], F32, name="z%d" % h) for h in range(2)]
@@ -227,4 +231,8 @@ def tile_residualblock5_pa_s_kernel(tc, x, k1, b1, gamma1, beta1, mean1, var1, o
                 out=result[h][:], in0=z[h][:], scalar=LEAKY_ALPHA, in1=z[h][:],
                 op0=ALU.mult, op1=ALU.max,
             )
-            nc.sync.dma_start(out=out_rows[:, half_cols[h]], in_=result[h][:])
+            for pos in range(POSITIONS):
+                store_by[pos].dma_start(
+                    out=out_by_pos[pos][:, half_cols[h]],
+                    in_=result[h][pos * BATCH : (pos + 1) * BATCH, :],
+                )

@@ -96,9 +96,6 @@ def tile_residualblock5_pa_s_kernel(tc, x, k1, b1, gamma1, beta1, mean1, var1, o
         scaled_bias = keep.tile([P, POSITIONS, CHUNKS], F32)
         shift_col = keep.tile([P, POSITIONS, CHUNKS], F32)
         vecT = psum.tile([P, P], BF16)
-        scale_ps = psum.tile([P, FILTERS], F32)
-        shift_ps = psum.tile([P, FILTERS], F32)
-        scale_sb = keep.tile([P, FILTERS], F32)
 
         def both_positions(col):
             return col.unsqueeze(1).to_broadcast([P, POSITIONS, CHUNKS])
@@ -127,44 +124,17 @@ def tile_residualblock5_pa_s_kernel(tc, x, k1, b1, gamma1, beta1, mean1, var1, o
                 out=shift_col[:], in0=scaled_bias[:], in1=both_positions(beta_col), op=ALU.add
             )
 
-        def spread_over_rows():
-            shift_rep = keep.tile([P, CHUNKS, POSITIONS, BATCH], F32)
-            nc.scalar.copy(
-                out=shift_rep[:],
-                in_=shift_col[:]
-                .rearrange("p l c -> p c l")
-                .unsqueeze(3)
-                .to_broadcast([P, CHUNKS, POSITIONS, BATCH]),
-            )
-            for c in range(CHUNKS):
-                nc.tensor.transpose(
-                    scale_ps[:, c * P : (c + 1) * P],
-                    scale_col[:, c : c + 1].to_broadcast([P, P]),
-                    ident_f32[:],
-                )
-            for c in range(CHUNKS):
-                nc.tensor.transpose(
-                    shift_ps[:, c * P : (c + 1) * P],
-                    shift_rep[:, c].rearrange("p l b -> p (l b)"),
-                    ident_f32[:],
-                )
-
-        def scale_into_sbuf():
-            nc.scalar.copy(out=scale_sb[:], in_=scale_ps[:])
-
         bn_stages = (
             vectors_onto_partitions,
             reciprocal_std,
             scale_and_centred_bias,
             scale_the_bias,
             add_beta,
-            spread_over_rows,
-            scale_into_sbuf,
         )
 
         w_codes = keep.tile([P, KERNELS, FILTERS], U32, align_bytes=64)
         w_scales = keep.tile([P, KERNELS, FILTERS], U8, align_bytes=64)
-        acc = [psum.tile([P, HALF], F32, name="acc%d" % h) for h in range(2)]
+        acc = [psum.tile([P, P], F32, name="acc%d" % c) for c in range(CHUNKS)]
         grouped = []
 
         def regroup(n):
@@ -186,19 +156,20 @@ def tile_residualblock5_pa_s_kernel(tc, x, k1, b1, gamma1, beta1, mean1, var1, o
 
         def multiply(n, h):
             tap, pos = divmod(n, POSITIONS)
-            cols = slice(h * HALF, (h + 1) * HALF)
             source = (pos - TAP_STEP[tap]) % POSITIONS
             first = (2 * source + 1 - pos) * BATCH
-            rows = slice(first, first + P)
-            nc.tensor.matmul_mx(
-                out=acc[h][:],
-                lhsT=x_codes[:, rows].bitcast(FP8X4),
-                lhsT_scale=x_scales[:, rows],
-                rhs=w_codes[:, n, cols].bitcast(FP8X4),
-                rhs_scale=w_scales[:, n, cols],
-                start=(n == 0),
-                stop=(n == KERNELS - 1),
-            )
+            window = slice(first, first + P)
+            for c in (2 * h, 2 * h + 1):
+                cols = slice(c * P, (c + 1) * P)
+                nc.tensor.matmul_mx(
+                    out=acc[c][:],
+                    lhsT=w_codes[:, n, cols].bitcast(FP8X4),
+                    lhsT_scale=w_scales[:, n, cols],
+                    rhs=x_codes[:, window].bitcast(FP8X4),
+                    rhs_scale=x_scales[:, window],
+                    start=(n == 0),
+                    stop=(n == KERNELS - 1),
+                )
 
         for n in range(KERNELS):
             regroup(n)
@@ -212,27 +183,43 @@ def tile_residualblock5_pa_s_kernel(tc, x, k1, b1, gamma1, beta1, mean1, var1, o
             quantise(KERNELS - 1, slice(h * HALF, (h + 1) * HALF))
             multiply(KERNELS - 1, h)
 
-        out_by_pos = out.rearrange("b l f -> l b f")
-        store_by = (nc.sync, nc.scalar)
-        half_cols = [slice(h * HALF, (h + 1) * HALF) for h in range(2)]
-        scaled = [keep.tile([P, HALF], F32, name="scaled%d" % h) for h in range(2)]
-        z = [keep.tile([P, HALF], F32, name="z%d" % h) for h in range(2)]
+        out_rows = out.rearrange("b l f -> (b l) f")
+        z = keep.tile([P, POSITIONS, CHUNKS, BATCH], F32)
+        leaky = keep.tile([P, CHUNKS, BATCH, POSITIONS], F32)
+        rows_ps = [psum.tile([P, HALF], F32, name="rows_ps%d" % h) for h in range(2)]
         result = [keep.tile([P, HALF], F32, name="result%d" % h) for h in range(2)]
+        for c in range(CHUNKS):
+            if c % 2 == 0:
+                nc.vector.scalar_tensor_tensor(
+                    out=z[:, :, c, :],
+                    in0=acc[c][:].rearrange("p (l b) -> p l b", l=POSITIONS),
+                    scalar=scale_col[:, c : c + 1],
+                    in1=shift_col[:, :, c : c + 1].to_broadcast([P, POSITIONS, BATCH]),
+                    op0=ALU.mult, op1=ALU.add,
+                )
+            else:
+                for pos in range(POSITIONS):
+                    nc.scalar.activation(
+                        out=z[:, pos, c, :],
+                        in_=acc[c][:, pos * BATCH : (pos + 1) * BATCH],
+                        func=ACT.Identity,
+                        scale=scale_col[:, c : c + 1],
+                        bias=shift_col[:, pos, c : c + 1],
+                    )
         for h in range(2):
-            nc.vector.tensor_tensor(
-                out=scaled[h][:], in0=acc[h][:], in1=scale_sb[:, half_cols[h]], op=ALU.mult
-            )
-        for h in range(2):
-            nc.vector.tensor_tensor(
-                out=z[h][:], in0=scaled[h][:], in1=shift_ps[:, half_cols[h]], op=ALU.add
-            )
-        for h in range(2):
+            pair = slice(2 * h, 2 * h + 2)
+            z_pair = z[:, :, pair, :].rearrange("p l c b -> p (c b) l")
             nc.vector.scalar_tensor_tensor(
-                out=result[h][:], in0=z[h][:], scalar=LEAKY_ALPHA, in1=z[h][:],
+                out=leaky[:, pair].rearrange("p c b l -> p (c b) l"),
+                in0=z_pair, scalar=LEAKY_ALPHA, in1=z_pair,
                 op0=ALU.mult, op1=ALU.max,
             )
-            for pos in range(POSITIONS):
-                store_by[pos].dma_start(
-                    out=out_by_pos[pos][:, half_cols[h]],
-                    in_=result[h][pos * BATCH : (pos + 1) * BATCH, :],
+        for h in range(2):
+            for j in range(2):
+                nc.tensor.transpose(
+                    rows_ps[h][:, j * P : (j + 1) * P],
+                    leaky[:, 2 * h + j].rearrange("p b l -> p (b l)"),
+                    ident_f32[:],
                 )
+            nc.scalar.copy(out=result[h][:], in_=rows_ps[h][:])
+            nc.sync.dma_start(out=out_rows[:, h * HALF : (h + 1) * HALF], in_=result[h][:])

@@ -139,9 +139,11 @@ def tile_residualblock5_pa_s_kernel(tc, x, k1, b1, gamma1, beta1, mean1, var1, o
 
         def regroup(n):
             grouped_n = keep.tile([P, FILTERS, PACK], BF16, name="grouped%d" % n, align_bytes=64)
-            for h in range(2):
-                cols = slice(h * HALF, (h + 1) * HALF)
-                copy_by[h](
+            shares = [(0, slice(0, HALF)), (1, slice(HALF, FILTERS))]
+            if n == KERNELS - 1:
+                shares = [(0, slice(0, HALF)), (1, slice(HALF, HALF + P)), (1, slice(HALF + P, FILTERS))]
+            for engine, cols in shares:
+                copy_by[engine](
                     out=grouped_n[:, cols, :].rearrange("p (c i) t -> p c t i", i=4),
                     in_=raw[n][:, :, cols].rearrange("p t (c i) -> p c t i", i=4),
                 )
@@ -154,12 +156,12 @@ def tile_residualblock5_pa_s_kernel(tc, x, k1, b1, gamma1, beta1, mean1, var1, o
                 in_=grouped[n][:, cols, :].rearrange("p f t -> p (f t)"),
             )
 
-        def multiply(n, h):
+        def multiply(n, chunks):
             tap, pos = divmod(n, POSITIONS)
             source = (pos - TAP_STEP[tap]) % POSITIONS
             first = (2 * source + 1 - pos) * BATCH
             window = slice(first, first + P)
-            for c in (2 * h, 2 * h + 1):
+            for c in chunks:
                 cols = slice(c * P, (c + 1) * P)
                 nc.tensor.matmul_mx(
                     out=acc[c][:],
@@ -175,51 +177,32 @@ def tile_residualblock5_pa_s_kernel(tc, x, k1, b1, gamma1, beta1, mean1, var1, o
             regroup(n)
             if n > 0:
                 quantise(n - 1, slice(0, FILTERS))
-                multiply(n - 1, 0)
-                multiply(n - 1, 1)
+                multiply(n - 1, range(CHUNKS))
             if BN_FIRST <= n < BN_FIRST + len(bn_stages):
                 bn_stages[n - BN_FIRST]()
-        for h in range(2):
-            quantise(KERNELS - 1, slice(h * HALF, (h + 1) * HALF))
-            multiply(KERNELS - 1, h)
+        for chunks in ((0, 1), (2,), (3,)):
+            quantise(KERNELS - 1, slice(chunks[0] * P, (chunks[-1] + 1) * P))
+            multiply(KERNELS - 1, chunks)
 
         out_rows = out.rearrange("b l f -> (b l) f")
-        z = keep.tile([P, POSITIONS, CHUNKS, BATCH], F32)
-        leaky = keep.tile([P, CHUNKS, BATCH, POSITIONS], F32)
-        rows_ps = [psum.tile([P, HALF], F32, name="rows_ps%d" % h) for h in range(2)]
-        result = [keep.tile([P, HALF], F32, name="result%d" % h) for h in range(2)]
         for c in range(CHUNKS):
-            if c % 2 == 0:
-                nc.vector.scalar_tensor_tensor(
-                    out=z[:, :, c, :],
-                    in0=acc[c][:].rearrange("p (l b) -> p l b", l=POSITIONS),
-                    scalar=scale_col[:, c : c + 1],
-                    in1=shift_col[:, :, c : c + 1].to_broadcast([P, POSITIONS, BATCH]),
-                    op0=ALU.mult, op1=ALU.add,
+            z = keep.tile([P, POSITIONS, BATCH], F32, name="z%d" % c)
+            for pos in range(POSITIONS):
+                nc.scalar.activation(
+                    out=z[:, pos, :],
+                    in_=acc[c][:, pos * BATCH : (pos + 1) * BATCH],
+                    func=ACT.Identity,
+                    scale=scale_col[:, c : c + 1],
+                    bias=shift_col[:, pos, c : c + 1],
                 )
-            else:
-                for pos in range(POSITIONS):
-                    nc.scalar.activation(
-                        out=z[:, pos, c, :],
-                        in_=acc[c][:, pos * BATCH : (pos + 1) * BATCH],
-                        func=ACT.Identity,
-                        scale=scale_col[:, c : c + 1],
-                        bias=shift_col[:, pos, c : c + 1],
-                    )
-        for h in range(2):
-            pair = slice(2 * h, 2 * h + 2)
-            z_pair = z[:, :, pair, :].rearrange("p l c b -> p (c b) l")
+            leaky = keep.tile([P, BATCH, POSITIONS], F32, name="leaky%d" % c)
+            z_by_row = z[:].rearrange("p l b -> p b l")
             nc.vector.scalar_tensor_tensor(
-                out=leaky[:, pair].rearrange("p c b l -> p (c b) l"),
-                in0=z_pair, scalar=LEAKY_ALPHA, in1=z_pair,
+                out=leaky[:], in0=z_by_row, scalar=LEAKY_ALPHA, in1=z_by_row,
                 op0=ALU.mult, op1=ALU.max,
             )
-        for h in range(2):
-            for j in range(2):
-                nc.tensor.transpose(
-                    rows_ps[h][:, j * P : (j + 1) * P],
-                    leaky[:, 2 * h + j].rearrange("p b l -> p (b l)"),
-                    ident_f32[:],
-                )
-            nc.scalar.copy(out=result[h][:], in_=rows_ps[h][:])
-            nc.sync.dma_start(out=out_rows[:, h * HALF : (h + 1) * HALF], in_=result[h][:])
+            rows_ps = psum.tile([P, P], F32, name="acc%d" % c)
+            nc.tensor.transpose(rows_ps[:], leaky[:].rearrange("p b l -> p (b l)"), ident_f32[:])
+            result = keep.tile([P, P], F32, name="result%d" % c)
+            nc.scalar.copy(out=result[:], in_=rows_ps[:])
+            nc.sync.dma_start(out=out_rows[:, c * P : (c + 1) * P], in_=result[:])

@@ -22,6 +22,7 @@ FLOPS = 2 * BATCH * POSITIONS * TAPS * CHANNELS * FILTERS
 
 KERNELS = TAPS * POSITIONS
 HALF = FILTERS // 2
+VECTOR_FILTERS = 240
 CHUNKS = FILTERS // P
 X_BLOCKS = 2 * POSITIONS + 1
 BN_FIRST = 2
@@ -139,7 +140,7 @@ def tile_residualblock5_pa_s_kernel(tc, x, k1, b1, gamma1, beta1, mean1, var1, o
 
         def regroup(n):
             grouped_n = keep.tile([P, FILTERS, PACK], BF16, name="grouped%d" % n, align_bytes=64)
-            shares = [(0, slice(0, HALF)), (1, slice(HALF, FILTERS))]
+            shares = [(0, slice(0, VECTOR_FILTERS)), (1, slice(VECTOR_FILTERS, FILTERS))]
             if n == KERNELS - 1:
                 shares = [(0, slice(0, HALF)), (1, slice(HALF, HALF + P)), (1, slice(HALF + P, FILTERS))]
             for engine, cols in shares:

@@ -145,8 +145,8 @@ def tile_residualblock5_pa_s_kernel(tc, x, k1, b1, gamma1, beta1, mean1, var1, o
                 shares = [(0, slice(0, HALF)), (1, slice(HALF, HALF + P)), (1, slice(HALF + P, FILTERS))]
             for engine, cols in shares:
                 copy_by[engine](
-                    out=grouped_n[:, cols, :].rearrange("p (c i) t -> p c t i", i=4),
-                    in_=raw[n][:, :, cols].rearrange("p t (c i) -> p c t i", i=4),
+                    out=grouped_n[:, cols, :].rearrange("p (c i) t -> p c t i", i=8),
+                    in_=raw[n][:, :, cols].rearrange("p t (c i) -> p c t i", i=8),
                 )
             grouped.append(grouped_n)
 

@@ -59,12 +59,12 @@ def tile_residualblock5_pa_s_kernel(tc, x, k1, b1, gamma1, beta1, mean1, var1, o
         nc.scalar.dma_start(
             out=vec_rows[4 * CHUNKS : 6 * CHUNKS, :], in_=b1.rearrange("l (c p) -> (l c) p", p=P)
         )
-        x_rows = keep.tile([P, CHANNELS], BF16)
+        x_rows = keep.tile([P, CHANNELS], BF16, align_bytes=256)
         nc.sync.dma_start(out=x_rows[:], in_=x.rearrange("b l c -> (b l) c"))
         raw = []
         for n in range(KERNELS):
             tap, pos = divmod(n, POSITIONS)
-            raw_n = keep.tile([P, PACK, FILTERS], BF16, name="raw%d" % n)
+            raw_n = keep.tile([P, PACK, FILTERS], BF16, name="raw%d" % n, align_bytes=256)
             nc.sync.dma_start(out=raw_n[:], in_=k1[tap, pos].rearrange("(p t) f -> p t f", t=PACK))
             raw.append(raw_n)
         warm = keep.tile([P, 1], F32)
@@ -204,6 +204,6 @@ def tile_residualblock5_pa_s_kernel(tc, x, k1, b1, gamma1, beta1, mean1, var1, o
             )
             rows_ps = psum.tile([P, P], F32, name="acc%d" % c)
             nc.tensor.transpose(rows_ps[:], leaky[:].rearrange("p b l -> p (b l)"), ident_f32[:])
-            result = keep.tile([P, P], F32, name="result%d" % c)
+            result = keep.tile([P, P], F32, name="result%d" % c, align_bytes=256)
             nc.scalar.copy(out=result[:], in_=rows_ps[:])
             nc.sync.dma_start(out=out_rows[:, c * P : (c + 1) * P], in_=result[:])

@@ -142,7 +142,12 @@ def tile_residualblock5_pa_s_kernel(tc, x, k1, b1, gamma1, beta1, mean1, var1, o
             grouped_n = keep.tile([P, FILTERS, PACK], BF16, name="grouped%d" % n, align_bytes=64)
             shares = [(0, slice(0, VECTOR_FILTERS)), (1, slice(VECTOR_FILTERS, FILTERS))]
             if n == KERNELS - 1:
-                shares = [(0, slice(0, HALF)), (1, slice(HALF, HALF + P)), (1, slice(HALF + P, FILTERS))]
+                shares = [
+                    (0, slice(0, HALF - BATCH)),
+                    (1, slice(HALF - BATCH, HALF)),
+                    (1, slice(HALF, HALF + P)),
+                    (1, slice(HALF + P, FILTERS)),
+                ]
             for engine, cols in shares:
                 copy_by[engine](
                     out=grouped_n[:, cols, :].rearrange("p (c i) t -> p c t i", i=8),

@@ -211,4 +211,5 @@ def tile_residualblock5_pa_s_kernel(tc, x, k1, b1, gamma1, beta1, mean1, var1, o
             nc.tensor.transpose(rows_ps[:], leaky[:].rearrange("p b l -> p (b l)"), ident_f32[:])
             result = keep.tile([P, P], F32, name="result%d" % c, align_bytes=256)
             nc.scalar.copy(out=result[:], in_=rows_ps[:])
-            nc.sync.dma_start(out=out_rows[:, c * P : (c + 1) * P], in_=result[:])
+            store_by = nc.scalar if c == CHUNKS - 1 else nc.sync
+            store_by.dma_start(out=out_rows[:, c * P : (c + 1) * P], in_=result[:])

@@ -43,10 +43,10 @@ def tile_residualblock5_pa_s_kernel(tc, x, k1, b1, gamma1, beta1, mean1, var1, o
         make_identity(nc, ident_f32[:])
         one = keep.tile([P, 1], F32)
         nc.vector.memset(one[:], 1.0)
-        x_grouped = keep.tile([P, POSITIONS, 2, BATCH * PACK], BF16, align_bytes=64)
+        x_grouped = keep.tile([P, POSITIONS, 2, BATCH * PACK], BF16, align_bytes=256)
         nc.gpsimd.memset(x_grouped[:, :, 0, :], 0.0)
-        x_codes = keep.tile([P, X_BLOCKS * BATCH], U32, align_bytes=64)
-        x_scales = keep.tile([P, X_BLOCKS * BATCH], U8, align_bytes=64)
+        x_codes = keep.tile([P, X_BLOCKS * BATCH], U32, align_bytes=256)
+        x_scales = keep.tile([P, X_BLOCKS * BATCH], U8, align_bytes=256)
         last_block = slice((X_BLOCKS - 1) * BATCH, X_BLOCKS * BATCH)
         nc.vector.memset(x_codes[:, last_block].bitcast(I32), 0)
         nc.vector.memset(x_scales[:, last_block].bitcast(I32), 0)
@@ -133,13 +133,13 @@ def tile_residualblock5_pa_s_kernel(tc, x, k1, b1, gamma1, beta1, mean1, var1, o
             add_beta,
         )
 
-        w_codes = keep.tile([P, KERNELS, FILTERS], U32, align_bytes=64)
-        w_scales = keep.tile([P, KERNELS, FILTERS], U8, align_bytes=64)
+        w_codes = keep.tile([P, KERNELS, FILTERS], U32, align_bytes=256)
+        w_scales = keep.tile([P, KERNELS, FILTERS], U8, align_bytes=256)
         acc = [psum.tile([P, P], F32, name="acc%d" % c) for c in range(CHUNKS)]
         grouped = []
 
         def regroup(n):
-            grouped_n = keep.tile([P, FILTERS, PACK], BF16, name="grouped%d" % n, align_bytes=64)
+            grouped_n = keep.tile([P, FILTERS, PACK], BF16, name="grouped%d" % n, align_bytes=256)
             shares = [(0, slice(0, VECTOR_FILTERS)), (1, slice(VECTOR_FILTERS, FILTERS))]
             if n == KERNELS - 1:
                 shares = [

from contextlib import ExitStack

import concourse.mybir as mybir
from concourse.masks import make_identity

BF16 = mybir.dt.bfloat16
F32 = mybir.dt.float32
U32 = mybir.dt.uint32
U8 = mybir.dt.uint8
I32 = mybir.dt.int32
FP8X4 = mybir.dt.float8_e4m3fn_x4
ALU = mybir.AluOpType
ACT = mybir.ActivationFunctionType

P = 128
PACK = 4
BATCH, POSITIONS, CHANNELS, FILTERS, TAPS = 64, 2, 512, 512, 5
TAP_STEP = (0, 0, 1, -1, 2)
BN_EPS = 1e-3
LEAKY_ALPHA = 0.3
FLOPS = 2 * BATCH * POSITIONS * TAPS * CHANNELS * FILTERS

KERNELS = TAPS * POSITIONS
HALF = FILTERS // 2
VECTOR_FILTERS = 240
CHUNKS = FILTERS // P
X_BLOCKS = 2 * POSITIONS + 1
BN_FIRST = 2


def tile_residualblock5_pa_s_kernel(tc, x, k1, b1, gamma1, beta1, mean1, var1, out):
    nc = tc.nc
    with ExitStack() as ctx:
        keep = ctx.enter_context(tc.tile_pool(name="keep", bufs=1))
        psum = ctx.enter_context(tc.psum_pool(name="psum", bufs=1))
        copy_by = (nc.vector.tensor_copy, nc.scalar.copy)

        vec_rows = keep.tile([P, P], BF16)
        nc.gpsimd.memset(vec_rows[:], 0.0)
        ident_bf16 = keep.tile([P, P], BF16)
        make_identity(nc, ident_bf16[:])
        ident_f32 = keep.tile([P, P], F32)
        make_identity(nc, ident_f32[:])
        one = keep.tile([P, 1], F32)
        nc.vector.memset(one[:], 1.0)
        x_grouped = keep.tile([P, POSITIONS, 2, BATCH * PACK], BF16, align_bytes=256)
        nc.gpsimd.memset(x_grouped[:, :, 0, :], 0.0)
        x_codes = keep.tile([P, X_BLOCKS * BATCH], U32, align_bytes=256)
        x_scales = keep.tile([P, X_BLOCKS * BATCH], U8, align_bytes=256)
        last_block = slice((X_BLOCKS - 1) * BATCH, X_BLOCKS * BATCH)
        nc.vector.memset(x_codes[:, last_block].bitcast(I32), 0)
        nc.vector.memset(x_scales[:, last_block].bitcast(I32), 0)

        for row, vec in enumerate((gamma1, beta1, mean1, var1)):
            nc.scalar.dma_start(
                out=vec_rows[row * CHUNKS : (row + 1) * CHUNKS, :],
                in_=vec.rearrange("(c p) -> c p", p=P),
            )
        nc.scalar.dma_start(
            out=vec_rows[4 * CHUNKS : 6 * CHUNKS, :], in_=b1.rearrange("l (c p) -> (l c) p", p=P)
        )
        x_rows = keep.tile([P, CHANNELS], BF16, align_bytes=256)
        nc.sync.dma_start(out=x_rows[:], in_=x.rearrange("b l c -> (b l) c"))
        raw = []
        for n in range(KERNELS):
            tap, pos = divmod(n, POSITIONS)
            raw_n = keep.tile([P, PACK, FILTERS], BF16, name="raw%d" % n, align_bytes=256)
            nc.sync.dma_start(out=raw_n[:], in_=k1[tap, pos].rearrange("(p t) f -> p t f", t=PACK))
            raw.append(raw_n)
        warm = keep.tile([P, 1], F32)
        nc.scalar.activation(out=warm[:], in_=one[:], func=ACT.Abs_reciprocal_sqrt)

        x_words = x_rows[:].bitcast(F32).rearrange("r (p u) -> r u p", u=2)
        xT = psum.tile([P, 2, P], F32)
        for u in range(2):
            nc.tensor.transpose(xT[:, u, :], x_words[:, u, :], ident_f32[:])
        nc.vector.tensor_copy(
            out=x_grouped[:, :, 1, :].bitcast(F32).rearrange("p l (b u) -> p l b u", u=2),
            in_=xT[:].rearrange("p u (b l) -> p l b u", l=POSITIONS),
        )
        quantised_blocks = slice(0, (X_BLOCKS - 1) * BATCH)
        nc.vector.quantize_mx(
            out=x_codes[:, quantised_blocks].bitcast(FP8X4),
            scales=x_scales[:, quantised_blocks],
            in_=x_grouped[:].rearrange("p l z c -> p (l z c)"),
        )

        vec_cols = keep.tile([P, 6 * CHUNKS], F32)
        gamma_col = vec_cols[:, 0 * CHUNKS : 1 * CHUNKS]
        beta_col = vec_cols[:, 1 * CHUNKS : 2 * CHUNKS]
        mean_col = vec_cols[:, 2 * CHUNKS : 3 * CHUNKS]
        var_col = vec_cols[:, 3 * CHUNKS : 4 * CHUNKS]
        bias_col = vec_cols[:, 4 * CHUNKS : 6 * CHUNKS].rearrange("p (l c) -> p l c", l=POSITIONS)
        rstd = keep.tile([P, CHUNKS], F32)
        scale_col = keep.tile([P, CHUNKS], F32)
        centred = keep.tile([P, POSITIONS, CHUNKS], F32)
        scaled_bias = keep.tile([P, POSITIONS, CHUNKS], F32)
        shift_col = keep.tile([P, POSITIONS, CHUNKS], F32)
        vecT = psum.tile([P, P], BF16)

        def both_positions(col):
            return col.unsqueeze(1).to_broadcast([P, POSITIONS, CHUNKS])

        def vectors_onto_partitions():
            nc.tensor.transpose(vecT[:], vec_rows[:], ident_bf16[:])

        def reciprocal_std():
            nc.scalar.copy(out=vec_cols[:], in_=vecT[:, 0 : 6 * CHUNKS])
            nc.scalar.activation(out=rstd[:], in_=var_col, func=ACT.Abs_reciprocal_sqrt, bias=BN_EPS)

        def scale_and_centred_bias():
            nc.vector.tensor_tensor(out=scale_col[:], in0=gamma_col, in1=rstd[:], op=ALU.mult)
            nc.vector.scalar_tensor_tensor(
                out=centred[:], in0=bias_col, scalar=2.0, in1=both_positions(mean_col),
                op0=ALU.mult, op1=ALU.subtract,
            )

        def scale_the_bias():
            nc.vector.tensor_tensor(
                out=scaled_bias[:], in0=centred[:], in1=both_positions(scale_col[:]), op=ALU.mult
            )

        def add_beta():
            nc.vector.tensor_tensor(
                out=shift_col[:], in0=scaled_bias[:], in1=both_positions(beta_col), op=ALU.add
            )

        bn_stages = (
            vectors_onto_partitions,
            reciprocal_std,
            scale_and_centred_bias,
            scale_the_bias,
            add_beta,
        )

        w_codes = keep.tile([P, KERNELS, FILTERS], U32, align_bytes=256)
        w_scales = keep.tile([P, KERNELS, FILTERS], U8, align_bytes=256)
        acc = [psum.tile([P, P], F32, name="acc%d" % c) for c in range(CHUNKS)]
        grouped = []

        def regroup(n):
            grouped_n = keep.tile([P, FILTERS, PACK], BF16, name="grouped%d" % n, align_bytes=256)
            shares = [(0, slice(0, VECTOR_FILTERS)), (1, slice(VECTOR_FILTERS, FILTERS))]
            if n == KERNELS - 1:
                shares = [
                    (0, slice(0, HALF - BATCH)),
                    (1, slice(HALF - BATCH, HALF)),
                    (1, slice(HALF, HALF + P)),
                    (1, slice(HALF + P, FILTERS)),
                ]
            for engine, cols in shares:
                copy_by[engine](
                    out=grouped_n[:, cols, :].rearrange("p (c i) t -> p c t i", i=8),
                    in_=raw[n][:, :, cols].rearrange("p t (c i) -> p c t i", i=8),
                )
            grouped.append(grouped_n)

        def quantise(n, cols):
            nc.vector.quantize_mx(
                out=w_codes[:, n, cols].bitcast(FP8X4),
                scales=w_scales[:, n, cols],
                in_=grouped[n][:, cols, :].rearrange("p f t -> p (f t)"),
            )

        def multiply(n, chunks):
            tap, pos = divmod(n, POSITIONS)
            source = (pos - TAP_STEP[tap]) % POSITIONS
            first = (2 * source + 1 - pos) * BATCH
            window = slice(first, first + P)
            for c in chunks:
                cols = slice(c * P, (c + 1) * P)
                nc.tensor.matmul_mx(
                    out=acc[c][:],
                    lhsT=w_codes[:, n, cols].bitcast(FP8X4),
                    lhsT_scale=w_scales[:, n, cols],
                    rhs=x_codes[:, window].bitcast(FP8X4),
                    rhs_scale=x_scales[:, window],
                    start=(n == 0),
                    stop=(n == KERNELS - 1),
                )

        for n in range(KERNELS):
            regroup(n)
            if n > 0:
                quantise(n - 1, slice(0, FILTERS))
                multiply(n - 1, range(CHUNKS))
            if BN_FIRST <= n < BN_FIRST + len(bn_stages):
                bn_stages[n - BN_FIRST]()
        for chunks in ((0, 1), (2,), (3,)):
            quantise(KERNELS - 1, slice(chunks[0] * P, (chunks[-1] + 1) * P))
            multiply(KERNELS - 1, chunks)

        out_rows = out.rearrange("b l f -> (b l) f")
        for c in range(CHUNKS):
            z = keep.tile([P, POSITIONS, BATCH], F32, name="z%d" % c)
            for pos in range(POSITIONS):
                nc.scalar.activation(
                    out=z[:, pos, :],
                    in_=acc[c][:, pos * BATCH : (pos + 1) * BATCH],
                    func=ACT.Identity,
                    scale=scale_col[:, c : c + 1],
                    bias=shift_col[:, pos, c : c + 1],
                )
            leaky = keep.tile([P, BATCH, POSITIONS], F32, name="leaky%d" % c)
            z_by_row = z[:].rearrange("p l b -> p b l")
            nc.vector.scalar_tensor_tensor(
                out=leaky[:], in0=z_by_row, scalar=LEAKY_ALPHA, in1=z_by_row,
                op0=ALU.mult, op1=ALU.max,
            )
            rows_ps = psum.tile([P, P], F32, name="acc%d" % c)
            nc.tensor.transpose(rows_ps[:], leaky[:].rearrange("p b l -> p (b l)"), ident_f32[:])
            result = keep.tile([P, P], F32, name="result%d" % c, align_bytes=256)
            nc.scalar.copy(out=result[:], in_=rows_ps[:])
            store_by = nc.scalar if c == CHUNKS - 1 else nc.sync
            store_by.dma_start(out=out_rows[:, c * P : (c + 1) * P], in_=result[:])
